import numpy as np
import ml_dtypes


def mxq(x, axis, fmt="e4m3"):
    dtype, down = {"e4m3": (ml_dtypes.float8_e4m3fn, 7), "e5m2": (ml_dtypes.float8_e5m2, 14)}[fmt]
    v = np.moveaxis(np.asarray(x, np.float32).astype(ml_dtypes.bfloat16).astype(np.float64), axis, -1)
    blocks = v.reshape(v.shape[:-1] + (-1, 32))
    amax = np.abs(blocks).max(-1, keepdims=True)
    byte = np.maximum(np.where(amax > 0, np.frexp(amax)[1] - 1 + 127, 0) - down, 1)
    scale = np.exp2(byte - 127.0)
    codes = (blocks / scale).astype(np.float32).astype(dtype).astype(np.float64)
    return np.moveaxis((codes * scale).reshape(v.shape), -1, axis)


WIDE = False


def mx_kscale(k):
    if not WIDE:
        return np.ones(k)
    levels = np.array([10, -10, 5, -5, 0])
    a = np.random.permutation(np.resize(levels, k // 512 * 4)).reshape(k // 512, 4)
    idx = np.arange(k)
    return np.exp2(a[idx // 512, idx % 128 // 32])


BF16 = ml_dtypes.bfloat16


def bf(x):
    return np.asarray(x, np.float32).astype(BF16)


def f64(x):
    return np.asarray(x).astype(np.float64)


B, C, V, K, OUT = 16, 128, 1024, 4, 128


def setup_inputs():
    s = mx_kscale(V)
    g = np.random.standard_normal((V, V))
    lap = (g + g.T) * (0.45 / np.sqrt(V))
    return {"input": bf(np.random.standard_normal((B, C, V)) * s),
            "laplacian": bf(lap * s[:, None] / s[None, :])}


def reference(input, laplacian):
    x0 = f64(input).transpose(2, 1, 0).reshape(V, C * B)
    lq = mxq(f64(laplacian), 1, "e4m3")
    x1 = lq @ mxq(x0, 0, "e4m3")
    x2 = 2.0 * (lq @ mxq(x1, 0, "e4m3")) - x0
    return x1, x2

@@ -1,0 +1,256 @@
+from contextlib import ExitStack
+
+import concourse.mybir as mybir
+from concourse.masks import make_identity
+
+F32 = mybir.dt.float32
+BF16 = mybir.dt.bfloat16
+U32 = mybir.dt.uint32
+U8 = mybir.dt.uint8
+FP8X4 = mybir.dt.float8_e4m3fn_x4
+ALU = mybir.AluOpType
+
+P = 128
+V = 1024
+N = 2048
+FLOPS = 2 * 2 * V * V * N
+
+PIECES = (4, 4, 4, 2, 2)
+
+
+def tile_graph_conv_pa_t_kernel(tc, signal, laplacian, out_0, out_1):
+    nc = tc.nc
+    with ExitStack() as ctx:
+        keep = ctx.enter_context(tc.tile_pool(name="keep", bufs=1))
+        lgp = ctx.enter_context(tc.tile_pool(name="lgp", bufs=2))
+        stage = ctx.enter_context(tc.tile_pool(name="stage", bufs=6))
+        x1gp = ctx.enter_context(tc.tile_pool(name="x1gp", bufs=3))
+        psum = ctx.enter_context(tc.psum_pool(name="psum", bufs=8))
+        ctx.enter_context(tc.manual_schedule())
+
+        ident = keep.tile([P, P], F32, name="ident")
+        make_identity(nc, ident[:])
+
+        lraw = [keep.tile([P, 2048], BF16, name="lraw%d" % a) for a in range(4)]
+        xraw = [keep.tile([P, nr * 1024], BF16, name="xraw%d" % i) for i, nr in enumerate(PIECES)]
+        x0g = [keep.tile([P, 4 * N], BF16, name="x0g%d" % g, align_bytes=64) for g in range(2)]
+        x0c = keep.tile([P, 2 * N], U32, name="x0c", align_bytes=64)
+        x0s = keep.tile([P, 2 * N], U8, name="x0s", align_bytes=64)
+        x1c = keep.tile([P, 2 * N], U32, name="x1c", align_bytes=64)
+        x1s = keep.tile([P, 2 * N], U8, name="x1s", align_bytes=64)
+        lc = keep.tile([P, 2048], U32, name="lc", align_bytes=64)
+        ls = keep.tile([P, 2048], U8, name="ls", align_bytes=64)
+
+        lap_rows = laplacian.rearrange("(a p e) u -> a p (e u)", a=4, p=P, e=2)
+        sig_rows = signal.rearrange("b (h r) v -> (b h) (r v)", h=8, r=16)
+
+        def load_lap(a):
+            nc.sync.dma_start(out=lraw[a][:], in_=lap_rows[a])
+
+        load_lap(0)
+        xwords = []
+        r0 = 0
+        for i, nr in enumerate(PIECES):
+            nc.sync.dma_start(out=xraw[i][:], in_=sig_rows[:, r0 * 1024:(r0 + nr) * 1024])
+            for rl in range(nr):
+                xwords.append((xraw[i][:].bitcast(F32), rl))
+            r0 += nr
+        for a in range(1, 4):
+            load_lap(a)
+
+        out_views = [o.rearrange("(gp uh p e) n -> gp uh p e n", gp=2, uh=2, p=P, e=2) for o in (out_0, out_1)]
+
+        def new_bank():
+            bank = psum.tile([P, 512], F32, name="bank", tag="bank")
+            return bank
+
+        lgs = {}
+
+        def lap_bank(a, g):
+            bank = new_bank()
+            words = lraw[a][:].bitcast(F32)
+            for u in range(2):
+                for e in range(2):
+                    off = e * 512 + (2 * g + u) * P
+                    slot = 2 * u + e
+                    nc.tensor.transpose(out=bank[:, slot * P:(slot + 1) * P], in_=words[:, off:off + P], identity=ident[:])
+            return bank
+
+        def lap_copy(copy, a, g, bank):
+            if g == 0:
+                lg = lgp.tile([P, 2048], BF16, name="lg", tag="lg", align_bytes=64)
+                lgs[a] = lg
+            dst = lgs[a][:].bitcast(F32)[:, g * 512:(g + 1) * 512].rearrange("q (x u) -> q x u", u=2)
+            src = bank[:].rearrange("q (u x) -> q x u", u=2)
+            copy(out=dst, in_=src)
+
+        def lap_quant(a):
+            nc.vector.quantize_mx(
+                out=lc[:, a * 512:(a + 1) * 512].bitcast(FP8X4),
+                scales=ls[:, a * 512:(a + 1) * 512],
+                in_=lgs[a][:],
+            )
+
+        def x_bank(k, g):
+            bank = new_bank()
+            for u in range(2):
+                for rr in range(2):
+                    words, rl = xwords[2 * k + rr]
+                    off = rl * 512 + (2 * g + u) * P
+                    slot = 2 * u + rr
+                    nc.tensor.transpose(out=bank[:, slot * P:(slot + 1) * P], in_=words[:, off:off + P], identity=ident[:])
+            return bank
+
+        def x_copy(copy, k, g, bank):
+            dst = x0g[g][:].bitcast(F32).rearrange("q (h x u) -> q h x u", h=8, x=256, u=2)[:, :, 32 * k:32 * k + 32, :]
+            src = bank[:].rearrange("q (u x h) -> q h x u", u=2, x=32, h=8)
+            copy(out=dst, in_=src)
+
+        def x_quant(j):
+            for h in range(8):
+                for g in range(2):
+                    c0 = h * 256 + j * 64
+                    nc.vector.quantize_mx(
+                        out=x0c[:, g * N + c0:g * N + c0 + 64].bitcast(FP8X4),
+                        scales=x0s[:, g * N + c0:g * N + c0 + 64],
+                        in_=x0g[g][:, 4 * c0:4 * c0 + 256],
+                    )
+
+        def mx_pass(bank, a, e, g, codes, scales, ch):
+            w = a * 512 + g * 256 + e * P
+            c = g * N + ch * 512
+            nc.tensor.matmul_mx(
+                out=bank[:],
+                lhsT=lc[:, w:w + P].bitcast(FP8X4),
+                lhsT_scale=ls[:, w:w + P],
+                rhs=codes[:, c:c + 512].bitcast(FP8X4),
+                rhs_scale=scales[:, c:c + 512],
+                start=(g == 0),
+                stop=(g == 1),
+            )
+
+        s_copy = nc.scalar.copy
+        v_copy = nc.vector.tensor_copy
+
+        b0 = lap_bank(0, 0)
+        lap_copy(s_copy, 0, 0, b0)
+        b1 = lap_bank(0, 1)
+        lap_copy(v_copy, 0, 1, b1)
+        lap_quant(0)
+        for k in range(8):
+            j = k // 2
+            if k == 6:
+                x_quant(2)
+            for g in range(2):
+                bank = x_bank(k, g)
+                if k < 6:
+                    eng = v_copy if (k % 2 == 1 and g == 0) else s_copy
+                elif k == 6:
+                    eng = s_copy
+                else:
+                    eng = v_copy if g == 1 else s_copy
+                x_copy(eng, k, g, bank)
+            if k % 2 == 1 and 1 <= j <= 2:
+                x_quant(j - 1)
+        x_quant(3)
+        for g in range(2):
+            bank = lap_bank(1, g)
+            lap_copy(s_copy, 1, g, bank)
+        lap_quant(1)
+
+        x1sb = {}
+        x1g = {}
+
+        def s1_tasks(n, ts):
+            gp, ch = n // 4, n % 4
+            if n not in x1sb:
+                st = stage.tile([P, 2048], F32, name="st", tag="st")
+                x1sb[n] = st
+            for t in ts:
+                bank = new_bank()
+                for g in range(2):
+                    mx_pass(bank, 2 * gp + t // 2, t % 2, g, x0c, x0s, ch)
+                nc.scalar.copy(out=x1sb[n][:, t * 512:(t + 1) * 512], in_=bank[:])
+
+        def s1_store(n):
+            gp, ch = n // 4, n % 4
+            for uh in range(2):
+                nc.sync.dma_start(
+                    out=out_views[0][gp, uh][:, :, ch * 512:(ch + 1) * 512],
+                    in_=x1sb[n][:, uh * 1024:(uh + 1) * 1024].rearrange("p (e n) -> p e n", e=2),
+                )
+
+        def regroup(n):
+            xg = x1gp.tile([P, 2048], BF16, name="xg", tag="xg", align_bytes=64)
+            x1g[n] = xg
+            nc.vector.tensor_copy(
+                out=xg[:].rearrange("p (c i t) -> p c t i", c=P, i=4, t=4),
+                in_=x1sb[n][:].rearrange("p (t c i) -> p c t i", t=4, c=P, i=4),
+            )
+
+        def x1_quant(n):
+            c = (n // 4) * N + (n % 4) * 512
+            nc.vector.quantize_mx(out=x1c[:, c:c + 512].bitcast(FP8X4), scales=x1s[:, c:c + 512], in_=x1g[n][:])
+
+        s1_tasks(0, (0, 1))
+        s1_tasks(1, (0, 1))
+        s1_tasks(0, (2, 3))
+        s1_store(0)
+        s1_tasks(1, (2, 3))
+        s1_store(1)
+        regroup(0)
+        for a in (2, 3):
+            bank = lap_bank(a, 0)
+            lap_copy(s_copy, a, 0, bank)
+            bank = lap_bank(a, 1)
+            lap_copy(v_copy, a, 1, bank)
+        regroup(1)
+        x1_quant(0)
+        lap_quant(2)
+        lap_quant(3)
+        for n in range(2, 8):
+            s1_tasks(n, (0, 1, 2, 3))
+            s1_store(n)
+            if n < 7:
+                regroup(n)
+                x1_quant(n - 1)
+
+        def s2_evict(mt, ch, bank, xt):
+            a, e = mt // 2, mt % 2
+            t = 2 * (a % 2) + e
+            nc.vector.scalar_tensor_tensor(
+                out=xt[:, ch * 512:(ch + 1) * 512],
+                in0=bank[:],
+                scalar=2.0,
+                in1=x0g[a // 2][:].rearrange("q (n t) -> q n t", t=4)[:, ch * 512:(ch + 1) * 512, t],
+                op0=ALU.mult,
+                op1=ALU.subtract,
+            )
+
+        def s2_store(mt, xt, c0, c1):
+            a, e = mt // 2, mt % 2
+            nc.sync.dma_start(out=out_views[1][a // 2, a % 2][:, e, c0:c1], in_=xt[:, c0:c1])
+
+        first = {}
+        for mt in range(2):
+            for ch in range(4):
+                bank = new_bank()
+                first[(mt, ch)] = bank
+                mx_pass(bank, mt // 2, mt % 2, 0, x1c, x1s, ch)
+        regroup(7)
+        x1_quant(6)
+        x1_quant(7)
+        for mt in range(8):
+            xt = stage.tile([P, 2048], F32, name="st", tag="st")
+            for ch in range(4):
+                if mt < 2:
+                    bank = first[(mt, ch)]
+                else:
+                    bank = new_bank()
+                    mx_pass(bank, mt // 2, mt % 2, 0, x1c, x1s, ch)
+                mx_pass(bank, mt // 2, mt % 2, 1, x1c, x1s, ch)
+                s2_evict(mt, ch, bank, xt)
+                if mt == 7:
+                    s2_store(mt, xt, ch * 512, (ch + 1) * 512)
+            if mt < 7:
+                s2_store(mt, xt, 0, N)

@@ -16,14 +16,17 @@ N = 2048
 FLOPS = 2 * 2 * V * V * N
 
 PIECES = (4, 4, 4, 2, 2)
+LAP_AT = (1, 1)
+SG = (9, 12, 15, 18, 21, 24, 27)
 
 
 def tile_graph_conv_pa_t_kernel(tc, signal, laplacian, out_0, out_1):
     nc = tc.nc
     with ExitStack() as ctx:
         keep = ctx.enter_context(tc.tile_pool(name="keep", bufs=1))
+        big = ctx.enter_context(tc.tile_pool(name="big", bufs=4))
         lgp = ctx.enter_context(tc.tile_pool(name="lgp", bufs=2))
-        stage = ctx.enter_context(tc.tile_pool(name="stage", bufs=6))
+        x2p = ctx.enter_context(tc.tile_pool(name="x2p", bufs=6))
         x1gp = ctx.enter_context(tc.tile_pool(name="x1gp", bufs=3))
         psum = ctx.enter_context(tc.psum_pool(name="psum", bufs=8))
         ctx.enter_context(tc.manual_schedule())
@@ -32,7 +35,7 @@ def tile_graph_conv_pa_t_kernel(tc, signal, laplacian, out_0, out_1):
         make_identity(nc, ident[:])
 
         lraw = [keep.tile([P, 2048], BF16, name="lraw%d" % a) for a in range(4)]
-        xraw = [keep.tile([P, nr * 1024], BF16, name="xraw%d" % i) for i, nr in enumerate(PIECES)]
+        xraw = [big.tile([P, 8192], BF16, name="xraw%d" % i, tag="big") for i in range(2)]
         x0g = [keep.tile([P, 4 * N], BF16, name="x0g%d" % g, align_bytes=64) for g in range(2)]
         x0c = keep.tile([P, 2 * N], U32, name="x0c", align_bytes=64)
         x0s = keep.tile([P, 2 * N], U8, name="x0s", align_bytes=64)
@@ -48,12 +51,10 @@ def tile_graph_conv_pa_t_kernel(tc, signal, laplacian, out_0, out_1):
             nc.sync.dma_start(out=lraw[a][:], in_=lap_rows[a])
 
         load_lap(0)
-        xwords = []
         r0 = 0
-        for i, nr in enumerate(PIECES):
-            nc.sync.dma_start(out=xraw[i][:], in_=sig_rows[:, r0 * 1024:(r0 + nr) * 1024])
-            for rl in range(nr):
-                xwords.append((xraw[i][:].bitcast(F32), rl))
+        for nr in PIECES:
+            half, rl = r0 // 8, r0 % 8
+            nc.sync.dma_start(out=xraw[half][:, rl * 1024:(rl + nr) * 1024], in_=sig_rows[:, r0 * 1024:(r0 + nr) * 1024])
             r0 += nr
         for a in range(1, 4):
             load_lap(a)
@@ -95,8 +96,9 @@ def tile_graph_conv_pa_t_kernel(tc, signal, laplacian, out_0, out_1):
             bank = new_bank()
             for u in range(2):
                 for rr in range(2):
-                    words, rl = xwords[2 * k + rr]
-                    off = rl * 512 + (2 * g + u) * P
+                    r = 2 * k + rr
+                    words = xraw[r // 8][:].bitcast(F32)
+                    off = (r % 8) * 512 + (2 * g + u) * P
                     slot = 2 * u + rr
                     nc.tensor.transpose(out=bank[:, slot * P:(slot + 1) * P], in_=words[:, off:off + P], identity=ident[:])
             return bank
@@ -106,8 +108,8 @@ def tile_graph_conv_pa_t_kernel(tc, signal, laplacian, out_0, out_1):
             src = bank[:].rearrange("q (u x h) -> q h x u", u=2, x=32, h=8)
             copy(out=dst, in_=src)
 
-        def x_quant(j):
-            for h in range(8):
+        def x_quant(j, hs):
+            for h in hs:
                 for g in range(2):
                     c0 = h * 256 + j * 64
                     nc.vector.quantize_mx(
@@ -132,125 +134,127 @@ def tile_graph_conv_pa_t_kernel(tc, signal, laplacian, out_0, out_1):
         s_copy = nc.scalar.copy
         v_copy = nc.vector.tensor_copy
 
+        ALL_H = tuple(range(8))
         b0 = lap_bank(0, 0)
         lap_copy(s_copy, 0, 0, b0)
         b1 = lap_bank(0, 1)
         lap_copy(v_copy, 0, 1, b1)
         lap_quant(0)
         for k in range(8):
-            j = k // 2
-            if k == 6:
-                x_quant(2)
             for g in range(2):
                 bank = x_bank(k, g)
-                if k < 6:
-                    eng = v_copy if (k % 2 == 1 and g == 0) else s_copy
-                elif k == 6:
-                    eng = s_copy
-                else:
-                    eng = v_copy if g == 1 else s_copy
-                x_copy(eng, k, g, bank)
-            if k % 2 == 1 and 1 <= j <= 2:
-                x_quant(j - 1)
-        x_quant(3)
-        for g in range(2):
-            bank = lap_bank(1, g)
-            lap_copy(s_copy, 1, g, bank)
-        lap_quant(1)
+                on_vector = (g == 0 and k in (1, 3, 5)) or (g == 1 and k in (6, 7))
+                x_copy(v_copy if on_vector else s_copy, k, g, bank)
+            if k == 1:
+                x_quant(0, ALL_H)
+            if k == 3:
+                x_quant(1, ALL_H)
+            if k == 6:
+                x_quant(2, (0, 1))
+        x_quant(3, (0, 1))
+        for ch in range(1, 4):
+            for j in (2, 3):
+                x_quant(j, (2 * ch, 2 * ch + 1))
+            if ch == 1:
+                for g in range(2):
+                    bank = lap_bank(1, g)
+                    lap_copy(s_copy, 1, g, bank)
+                lap_quant(1)
 
         x1sb = {}
         x1g = {}
 
-        def s1_tasks(n, ts):
-            gp, ch = n // 4, n % 4
-            if n not in x1sb:
-                st = stage.tile([P, 2048], F32, name="st", tag="st")
-                x1sb[n] = st
+        def s1_tasks(gp, ch, ts):
+            key = (gp, ch // 2)
+            if key not in x1sb:
+                pair = big.tile([P, 4096], F32, name="pair", tag="big")
+                x1sb[key] = pair
             for t in ts:
                 bank = new_bank()
                 for g in range(2):
                     mx_pass(bank, 2 * gp + t // 2, t % 2, g, x0c, x0s, ch)
-                nc.scalar.copy(out=x1sb[n][:, t * 512:(t + 1) * 512], in_=bank[:])
+                c = t * 1024 + (ch % 2) * 512
+                nc.scalar.copy(out=x1sb[key][:, c:c + 512], in_=bank[:])
 
-        def s1_store(n):
-            gp, ch = n // 4, n % 4
-            for uh in range(2):
-                nc.sync.dma_start(
-                    out=out_views[0][gp, uh][:, :, ch * 512:(ch + 1) * 512],
-                    in_=x1sb[n][:, uh * 1024:(uh + 1) * 1024].rearrange("p (e n) -> p e n", e=2),
-                )
+        def s1_store(gp, uh, c0, c1):
+            half = c0 // 1024
+            src = x1sb[(gp, half)][:, uh * 2048:(uh + 1) * 2048].rearrange("p (e n) -> p e n", e=2)
+            nc.sync.dma_start(out=out_views[0][gp, uh][:, :, c0:c1], in_=src[:, :, c0 - half * 1024:c1 - half * 1024])
 
-        def regroup(n):
-            xg = x1gp.tile([P, 2048], BF16, name="xg", tag="xg", align_bytes=64)
-            x1g[n] = xg
-            nc.vector.tensor_copy(
-                out=xg[:].rearrange("p (c i t) -> p c t i", c=P, i=4, t=4),
-                in_=x1sb[n][:].rearrange("p (t c i) -> p c t i", t=4, c=P, i=4),
+        def s1_store_row(gp, t, half):
+            nc.sync.dma_start(
+                out=out_views[0][gp, t // 2][:, t % 2, half * 1024:(half + 1) * 1024],
+                in_=x1sb[(gp, half)][:, t * 1024:(t + 1) * 1024],
             )
 
-        def x1_quant(n):
-            c = (n // 4) * N + (n % 4) * 512
-            nc.vector.quantize_mx(out=x1c[:, c:c + 512].bitcast(FP8X4), scales=x1s[:, c:c + 512], in_=x1g[n][:])
+        def regroup(gp, ch, copy):
+            xg = x1gp.tile([P, 2048], BF16, name="xg", tag="xg", align_bytes=64)
+            x1g[(gp, ch)] = xg
+            src = x1sb[(gp, ch // 2)][:].rearrange("p (t n) -> p t n", t=4)[:, :, (ch % 2) * 512:(ch % 2) * 512 + 512]
+            copy(
+                out=xg[:].rearrange("p (c i t) -> p c t i", c=P, i=4, t=4),
+                in_=src.rearrange("p t (c i) -> p c t i", c=P, i=4),
+            )
 
-        s1_tasks(0, (0, 1))
-        s1_tasks(1, (0, 1))
-        s1_tasks(0, (2, 3))
-        s1_store(0)
-        s1_tasks(1, (2, 3))
-        s1_store(1)
-        regroup(0)
-        for a in (2, 3):
-            bank = lap_bank(a, 0)
-            lap_copy(s_copy, a, 0, bank)
-            bank = lap_bank(a, 1)
-            lap_copy(v_copy, a, 1, bank)
-        regroup(1)
-        x1_quant(0)
-        lap_quant(2)
-        lap_quant(3)
-        for n in range(2, 8):
-            s1_tasks(n, (0, 1, 2, 3))
-            s1_store(n)
-            if n < 7:
-                regroup(n)
-                x1_quant(n - 1)
+        def x1_quant(gp, ch):
+            c = gp * N + ch * 512
+            nc.vector.quantize_mx(out=x1c[:, c:c + 512].bitcast(FP8X4), scales=x1s[:, c:c + 512], in_=x1g[(gp, ch)][:])
 
-        def s2_evict(mt, ch, bank, xt):
+        def lap_late():
+            for a in (2, 3):
+                bank = lap_bank(a, 0)
+                lap_copy(s_copy, a, 0, bank)
+                bank = lap_bank(a, 1)
+                lap_copy(v_copy, a, 1, bank)
+            lap_quant(2)
+            lap_quant(3)
+
+        pairs = [(0, 0), (0, 1), (1, 0), (1, 1)]
+        for i, (gp, half) in enumerate(pairs):
+            for t in range(4):
+                for cc in range(2):
+                    s1_tasks(gp, 2 * half + cc, (t,))
+                s1_store_row(gp, t, half)
+                if i == LAP_AT[0] and t == LAP_AT[1]:
+                    lap_late()
+            if i < 3:
+                for cc in range(2):
+                    regroup(gp, 2 * half + cc, v_copy)
+                for cc in range(2):
+                    x1_quant(gp, 2 * half + cc)
+
+        def s2_evict(i, mt, ch, bank, res):
             a, e = mt // 2, mt % 2
             t = 2 * (a % 2) + e
-            nc.vector.scalar_tensor_tensor(
-                out=xt[:, ch * 512:(ch + 1) * 512],
-                in0=bank[:],
-                scalar=2.0,
-                in1=x0g[a // 2][:].rearrange("q (n t) -> q n t", t=4)[:, ch * 512:(ch + 1) * 512, t],
-                op0=ALU.mult,
-                op1=ALU.subtract,
-            )
+            x0t = x0g[a // 2][:].rearrange("q (n t) -> q n t", t=4)[:, ch * 512:(ch + 1) * 512, t]
+            if i in SG:
+                nc.scalar.mul(out=res, in_=bank[:], mul=2.0)
+                nc.gpsimd.tensor_tensor(out=res, in0=res, in1=x0t, op=ALU.subtract)
+            else:
+                nc.vector.scalar_tensor_tensor(out=res, in0=bank[:], scalar=2.0, in1=x0t, op0=ALU.mult, op1=ALU.subtract)
 
-        def s2_store(mt, xt, c0, c1):
+        def s2_store(mt, xt, half, c0, c1):
             a, e = mt // 2, mt % 2
-            nc.sync.dma_start(out=out_views[1][a // 2, a % 2][:, e, c0:c1], in_=xt[:, c0:c1])
+            nc.sync.dma_start(out=out_views[1][a // 2, a % 2][:, e, half * 1024 + c0:half * 1024 + c1], in_=xt[:, c0:c1])
 
-        first = {}
-        for mt in range(2):
-            for ch in range(4):
-                bank = new_bank()
-                first[(mt, ch)] = bank
-                mx_pass(bank, mt // 2, mt % 2, 0, x1c, x1s, ch)
-        regroup(7)
-        x1_quant(6)
-        x1_quant(7)
-        for mt in range(8):
-            xt = stage.tile([P, 2048], F32, name="st", tag="st")
-            for ch in range(4):
-                if mt < 2:
-                    bank = first[(mt, ch)]
-                else:
+        regroup(1, 2, s_copy)
+        regroup(1, 3, s_copy)
+        i = 0
+        for half in range(2):
+            for mt in range(8):
+                xt = x2p.tile([P, 1024], F32, name="xt", tag="xt")
+                for cc in range(2):
+                    ch = 2 * half + cc
                     bank = new_bank()
-                    mx_pass(bank, mt // 2, mt % 2, 0, x1c, x1s, ch)
-                mx_pass(bank, mt // 2, mt % 2, 1, x1c, x1s, ch)
-                s2_evict(mt, ch, bank, xt)
-                if mt == 7:
-                    s2_store(mt, xt, ch * 512, (ch + 1) * 512)
-            if mt < 7:
-                s2_store(mt, xt, 0, N)
+                    for g in range(2):
+                        mx_pass(bank, mt // 2, mt % 2, g, x1c, x1s, ch)
+                    s2_evict(i, mt, ch, bank, xt[:, cc * 512:(cc + 1) * 512])
+                    i += 1
+                    if half == 1 and mt == 7:
+                        s2_store(mt, xt, half, cc * 512, (cc + 1) * 512)
+                if not (half == 1 and mt == 7):
+                    s2_store(mt, xt, half, 0, 1024)
+                if half == 0 and mt == 3:
+                    x1_quant(1, 2)
+                if half == 0 and mt == 5:
+                    x1_quant(1, 3)

@@ -17,6 +17,7 @@ FLOPS = 2 * 2 * V * V * N
 
 PIECES = (4, 4, 4, 2, 2)
 LAP_AT = (1, 1)
+WARM = (0, 3, 0, 3, 0, 0, 1, 2)
 SG = (9, 12, 15, 18, 21, 24, 27)
 
 
@@ -33,6 +34,8 @@ def tile_graph_conv_pa_t_kernel(tc, signal, laplacian, out_0, out_1):
 
         ident = keep.tile([P, P], F32, name="ident")
         make_identity(nc, ident[:])
+        zeros = keep.tile([P, 512], BF16, name="zeros")
+        nc.vector.memset(zeros[:], 0.0)
 
         lraw = [keep.tile([P, 2048], BF16, name="lraw%d" % a) for a in range(4)]
         xraw = [big.tile([P, 8192], BF16, name="xraw%d" % i, tag="big") for i in range(2)]
@@ -64,6 +67,11 @@ def tile_graph_conv_pa_t_kernel(tc, signal, laplacian, out_0, out_1):
         def new_bank():
             bank = psum.tile([P, 512], F32, name="bank", tag="bank")
             return bank
+
+        def warm(count):
+            bank = new_bank()
+            for rep in range(count):
+                nc.tensor.matmul(out=bank[:], lhsT=zeros[:, 0:P], rhs=zeros[:], start=True, stop=True)
 
         lgs = {}
 
@@ -135,11 +143,13 @@ def tile_graph_conv_pa_t_kernel(tc, signal, laplacian, out_0, out_1):
         v_copy = nc.vector.tensor_copy
 
         ALL_H = tuple(range(8))
+        warm(4)
         b0 = lap_bank(0, 0)
         lap_copy(s_copy, 0, 0, b0)
         b1 = lap_bank(0, 1)
         lap_copy(v_copy, 0, 1, b1)
         lap_quant(0)
+        warm(3)
         for k in range(8):
             for g in range(2):
                 bank = x_bank(k, g)
@@ -151,6 +161,8 @@ def tile_graph_conv_pa_t_kernel(tc, signal, laplacian, out_0, out_1):
                 x_quant(1, ALL_H)
             if k == 6:
                 x_quant(2, (0, 1))
+            if WARM[k] > 0:
+                warm(WARM[k])
         x_quant(3, (0, 1))
         for ch in range(1, 4):
             for j in (2, 3):

@@ -17,8 +17,9 @@ FLOPS = 2 * 2 * V * V * N
 
 PIECES = (4, 4, 4, 2, 2)
 LAP_AT = (1, 1)
+V_EVICT = ()
 WARM = (0, 3, 0, 3, 0, 0, 1, 2)
-SG = (9, 12, 15, 18, 21, 24, 27)
+SG = (10, 15, 20, 25)
 
 
 def tile_graph_conv_pa_t_kernel(tc, signal, laplacian, out_0, out_1):
@@ -186,7 +187,8 @@ def tile_graph_conv_pa_t_kernel(tc, signal, laplacian, out_0, out_1):
                 for g in range(2):
                     mx_pass(bank, 2 * gp + t // 2, t % 2, g, x0c, x0s, ch)
                 c = t * 1024 + (ch % 2) * 512
-                nc.scalar.copy(out=x1sb[key][:, c:c + 512], in_=bank[:])
+                evict = v_copy if (t, ch % 2) in V_EVICT else s_copy
+                evict(out=x1sb[key][:, c:c + 512], in_=bank[:])
 
         def s1_store(gp, uh, c0, c1):
             half = c0 // 1024

@@ -28,7 +28,6 @@ def tile_graph_conv_pa_t_kernel(tc, signal, laplacian, out_0, out_1):
         keep = ctx.enter_context(tc.tile_pool(name="keep", bufs=1))
         big = ctx.enter_context(tc.tile_pool(name="big", bufs=4))
         lgp = ctx.enter_context(tc.tile_pool(name="lgp", bufs=2))
-        x2p = ctx.enter_context(tc.tile_pool(name="x2p", bufs=6))
         x1gp = ctx.enter_context(tc.tile_pool(name="x1gp", bufs=3))
         psum = ctx.enter_context(tc.psum_pool(name="psum", bufs=8))
         ctx.enter_context(tc.manual_schedule())
@@ -195,11 +194,13 @@ def tile_graph_conv_pa_t_kernel(tc, signal, laplacian, out_0, out_1):
             src = x1sb[(gp, half)][:, uh * 2048:(uh + 1) * 2048].rearrange("p (e n) -> p e n", e=2)
             nc.sync.dma_start(out=out_views[0][gp, uh][:, :, c0:c1], in_=src[:, :, c0 - half * 1024:c1 - half * 1024])
 
-        def s1_store_row(gp, t, half):
-            nc.sync.dma_start(
-                out=out_views[0][gp, t // 2][:, t % 2, half * 1024:(half + 1) * 1024],
-                in_=x1sb[(gp, half)][:, t * 1024:(t + 1) * 1024],
-            )
+        def store_rows(which, unit, gp, half, t, count, c0=0, c1=1024):
+            cols = slice(half * 1024 + c0, half * 1024 + c1)
+            if count == 1:
+                nc.sync.dma_start(out=out_views[which][gp, t // 2][:, t % 2, cols], in_=unit[:, t * 1024 + c0:t * 1024 + c1])
+            else:
+                src = unit[:, t * 1024:(t + 2) * 1024].rearrange("p (e n) -> p e n", e=2)
+                nc.sync.dma_start(out=out_views[which][gp, t // 2][:, :, cols], in_=src[:, :, c0:c1])
 
         def regroup(gp, ch, copy):
             xg = x1gp.tile([P, 2048], BF16, name="xg", tag="xg", align_bytes=64)
@@ -228,7 +229,10 @@ def tile_graph_conv_pa_t_kernel(tc, signal, laplacian, out_0, out_1):
             for t in range(4):
                 for cc in range(2):
                     s1_tasks(gp, 2 * half + cc, (t,))
-                s1_store_row(gp, t, half)
+                if i == 0:
+                    store_rows(0, x1sb[(gp, half)], gp, half, t, 1)
+                elif t % 2 == 1:
+                    store_rows(0, x1sb[(gp, half)], gp, half, t - 1, 2)
                 if i == LAP_AT[0] and t == LAP_AT[1]:
                     lap_late()
             if i < 3:
@@ -247,28 +251,30 @@ def tile_graph_conv_pa_t_kernel(tc, signal, laplacian, out_0, out_1):
             else:
                 nc.vector.scalar_tensor_tensor(out=res, in0=bank[:], scalar=2.0, in1=x0t, op0=ALU.mult, op1=ALU.subtract)
 
-        def s2_store(mt, xt, half, c0, c1):
-            a, e = mt // 2, mt % 2
-            nc.sync.dma_start(out=out_views[1][a // 2, a % 2][:, e, half * 1024 + c0:half * 1024 + c1], in_=xt[:, c0:c1])
-
         regroup(1, 2, s_copy)
         regroup(1, 3, s_copy)
         i = 0
         for half in range(2):
-            for mt in range(8):
-                xt = x2p.tile([P, 1024], F32, name="xt", tag="xt")
-                for cc in range(2):
-                    ch = 2 * half + cc
-                    bank = new_bank()
-                    for g in range(2):
-                        mx_pass(bank, mt // 2, mt % 2, g, x1c, x1s, ch)
-                    s2_evict(i, mt, ch, bank, xt[:, cc * 512:(cc + 1) * 512])
-                    i += 1
-                    if half == 1 and mt == 7:
-                        s2_store(mt, xt, half, cc * 512, (cc + 1) * 512)
-                if not (half == 1 and mt == 7):
-                    s2_store(mt, xt, half, 0, 1024)
-                if half == 0 and mt == 3:
-                    x1_quant(1, 2)
-                if half == 0 and mt == 5:
-                    x1_quant(1, 3)
+            for gp in range(2):
+                unit = big.tile([P, 4096], F32, name="unit", tag="big")
+                last = half == 1 and gp == 1
+                for t in range(4):
+                    mt = 4 * gp + t
+                    for cc in range(2):
+                        ch = 2 * half + cc
+                        bank = new_bank()
+                        for g in range(2):
+                            mx_pass(bank, mt // 2, mt % 2, g, x1c, x1s, ch)
+                        c = t * 1024 + cc * 512
+                        s2_evict(i, mt, ch, bank, unit[:, c:c + 512])
+                        i += 1
+                        if last and t == 3:
+                            store_rows(1, unit, gp, half, t, 1, cc * 512, (cc + 1) * 512)
+                    if last and t == 2:
+                        store_rows(1, unit, gp, half, t, 1)
+                    elif t % 2 == 1 and not (last and t == 3):
+                        store_rows(1, unit, gp, half, t - 1, 2)
+                    if half == 0 and mt == 3:
+                        x1_quant(1, 2)
+                    if half == 0 and mt == 5:
+                        x1_quant(1, 3)

from contextlib import ExitStack

import concourse.mybir as mybir
from concourse.masks import make_identity

F32 = mybir.dt.float32
BF16 = mybir.dt.bfloat16
U32 = mybir.dt.uint32
U8 = mybir.dt.uint8
FP8X4 = mybir.dt.float8_e4m3fn_x4
ALU = mybir.AluOpType

P = 128
V = 1024
N = 2048
FLOPS = 2 * 2 * V * V * N

PIECES = (4, 4, 4, 2, 2)
LAP_AT = (1, 1)
V_EVICT = ()
WARM = (0, 3, 0, 3, 0, 0, 1, 2)
SG = (10, 15, 20, 25)


def tile_graph_conv_pa_t_kernel(tc, signal, laplacian, out_0, out_1):
    nc = tc.nc
    with ExitStack() as ctx:
        keep = ctx.enter_context(tc.tile_pool(name="keep", bufs=1))
        big = ctx.enter_context(tc.tile_pool(name="big", bufs=4))
        lgp = ctx.enter_context(tc.tile_pool(name="lgp", bufs=2))
        x1gp = ctx.enter_context(tc.tile_pool(name="x1gp", bufs=3))
        psum = ctx.enter_context(tc.psum_pool(name="psum", bufs=8))
        ctx.enter_context(tc.manual_schedule())

        ident = keep.tile([P, P], F32, name="ident")
        make_identity(nc, ident[:])
        zeros = keep.tile([P, 512], BF16, name="zeros")
        nc.vector.memset(zeros[:], 0.0)

        lraw = [keep.tile([P, 2048], BF16, name="lraw%d" % a) for a in range(4)]
        xraw = [big.tile([P, 8192], BF16, name="xraw%d" % i, tag="big") for i in range(2)]
        x0g = [keep.tile([P, 4 * N], BF16, name="x0g%d" % g, align_bytes=64) for g in range(2)]
        x0c = keep.tile([P, 2 * N], U32, name="x0c", align_bytes=64)
        x0s = keep.tile([P, 2 * N], U8, name="x0s", align_bytes=64)
        x1c = keep.tile([P, 2 * N], U32, name="x1c", align_bytes=64)
        x1s = keep.tile([P, 2 * N], U8, name="x1s", align_bytes=64)
        lc = keep.tile([P, 2048], U32, name="lc", align_bytes=64)
        ls = keep.tile([P, 2048], U8, name="ls", align_bytes=64)

        lap_rows = laplacian.rearrange("(a p e) u -> a p (e u)", a=4, p=P, e=2)
        sig_rows = signal.rearrange("b (h r) v -> (b h) (r v)", h=8, r=16)

        def load_lap(a):
            nc.sync.dma_start(out=lraw[a][:], in_=lap_rows[a])

        load_lap(0)
        r0 = 0
        for nr in PIECES:
            half, rl = r0 // 8, r0 % 8
            nc.sync.dma_start(out=xraw[half][:, rl * 1024:(rl + nr) * 1024], in_=sig_rows[:, r0 * 1024:(r0 + nr) * 1024])
            r0 += nr
        for a in range(1, 4):
            load_lap(a)

        out_views = [o.rearrange("(gp uh p e) n -> gp uh p e n", gp=2, uh=2, p=P, e=2) for o in (out_0, out_1)]

        def new_bank():
            bank = psum.tile([P, 512], F32, name="bank", tag="bank")
            return bank

        def warm(count):
            bank = new_bank()
            for rep in range(count):
                nc.tensor.matmul(out=bank[:], lhsT=zeros[:, 0:P], rhs=zeros[:], start=True, stop=True)

        lgs = {}

        def lap_bank(a, g):
            bank = new_bank()
            words = lraw[a][:].bitcast(F32)
            for u in range(2):
                for e in range(2):
                    off = e * 512 + (2 * g + u) * P
                    slot = 2 * u + e
                    nc.tensor.transpose(out=bank[:, slot * P:(slot + 1) * P], in_=words[:, off:off + P], identity=ident[:])
            return bank

        def lap_copy(copy, a, g, bank):
            if g == 0:
                lg = lgp.tile([P, 2048], BF16, name="lg", tag="lg", align_bytes=64)
                lgs[a] = lg
            dst = lgs[a][:].bitcast(F32)[:, g * 512:(g + 1) * 512].rearrange("q (x u) -> q x u", u=2)
            src = bank[:].rearrange("q (u x) -> q x u", u=2)
            copy(out=dst, in_=src)

        def lap_quant(a):
            nc.vector.quantize_mx(
                out=lc[:, a * 512:(a + 1) * 512].bitcast(FP8X4),
                scales=ls[:, a * 512:(a + 1) * 512],
                in_=lgs[a][:],
            )

        def x_bank(k, g):
            bank = new_bank()
            for u in range(2):
                for rr in range(2):
                    r = 2 * k + rr
                    words = xraw[r // 8][:].bitcast(F32)
                    off = (r % 8) * 512 + (2 * g + u) * P
                    slot = 2 * u + rr
                    nc.tensor.transpose(out=bank[:, slot * P:(slot + 1) * P], in_=words[:, off:off + P], identity=ident[:])
            return bank

        def x_copy(copy, k, g, bank):
            dst = x0g[g][:].bitcast(F32).rearrange("q (h x u) -> q h x u", h=8, x=256, u=2)[:, :, 32 * k:32 * k + 32, :]
            src = bank[:].rearrange("q (u x h) -> q h x u", u=2, x=32, h=8)
            copy(out=dst, in_=src)

        def x_quant(j, hs):
            for h in hs:
                for g in range(2):
                    c0 = h * 256 + j * 64
                    nc.vector.quantize_mx(
                        out=x0c[:, g * N + c0:g * N + c0 + 64].bitcast(FP8X4),
                        scales=x0s[:, g * N + c0:g * N + c0 + 64],
                        in_=x0g[g][:, 4 * c0:4 * c0 + 256],
                    )

        def mx_pass(bank, a, e, g, codes, scales, ch):
            w = a * 512 + g * 256 + e * P
            c = g * N + ch * 512
            nc.tensor.matmul_mx(
                out=bank[:],
                lhsT=lc[:, w:w + P].bitcast(FP8X4),
                lhsT_scale=ls[:, w:w + P],
                rhs=codes[:, c:c + 512].bitcast(FP8X4),
                rhs_scale=scales[:, c:c + 512],
                start=(g == 0),
                stop=(g == 1),
            )

        s_copy = nc.scalar.copy
        v_copy = nc.vector.tensor_copy

        ALL_H = tuple(range(8))
        warm(4)
        b0 = lap_bank(0, 0)
        lap_copy(s_copy, 0, 0, b0)
        b1 = lap_bank(0, 1)
        lap_copy(v_copy, 0, 1, b1)
        lap_quant(0)
        warm(3)
        for k in range(8):
            for g in range(2):
                bank = x_bank(k, g)
                on_vector = (g == 0 and k in (1, 3, 5)) or (g == 1 and k in (6, 7))
                x_copy(v_copy if on_vector else s_copy, k, g, bank)
            if k == 1:
                x_quant(0, ALL_H)
            if k == 3:
                x_quant(1, ALL_H)
            if k == 6:
                x_quant(2, (0, 1))
            if WARM[k] > 0:
                warm(WARM[k])
        x_quant(3, (0, 1))
        for ch in range(1, 4):
            for j in (2, 3):
                x_quant(j, (2 * ch, 2 * ch + 1))
            if ch == 1:
                for g in range(2):
                    bank = lap_bank(1, g)
                    lap_copy(s_copy, 1, g, bank)
                lap_quant(1)

        x1sb = {}
        x1g = {}

        def s1_tasks(gp, ch, ts):
            key = (gp, ch // 2)
            if key not in x1sb:
                pair = big.tile([P, 4096], F32, name="pair", tag="big")
                x1sb[key] = pair
            for t in ts:
                bank = new_bank()
                for g in range(2):
                    mx_pass(bank, 2 * gp + t // 2, t % 2, g, x0c, x0s, ch)
                c = t * 1024 + (ch % 2) * 512
                evict = v_copy if (t, ch % 2) in V_EVICT else s_copy
                evict(out=x1sb[key][:, c:c + 512], in_=bank[:])

        def s1_store(gp, uh, c0, c1):
            half = c0 // 1024
            src = x1sb[(gp, half)][:, uh * 2048:(uh + 1) * 2048].rearrange("p (e n) -> p e n", e=2)
            nc.sync.dma_start(out=out_views[0][gp, uh][:, :, c0:c1], in_=src[:, :, c0 - half * 1024:c1 - half * 1024])

        def store_rows(which, unit, gp, half, t, count, c0=0, c1=1024):
            cols = slice(half * 1024 + c0, half * 1024 + c1)
            if count == 1:
                nc.sync.dma_start(out=out_views[which][gp, t // 2][:, t % 2, cols], in_=unit[:, t * 1024 + c0:t * 1024 + c1])
            else:
                src = unit[:, t * 1024:(t + 2) * 1024].rearrange("p (e n) -> p e n", e=2)
                nc.sync.dma_start(out=out_views[which][gp, t // 2][:, :, cols], in_=src[:, :, c0:c1])

        def regroup(gp, ch, copy):
            xg = x1gp.tile([P, 2048], BF16, name="xg", tag="xg", align_bytes=64)
            x1g[(gp, ch)] = xg
            src = x1sb[(gp, ch // 2)][:].rearrange("p (t n) -> p t n", t=4)[:, :, (ch % 2) * 512:(ch % 2) * 512 + 512]
            copy(
                out=xg[:].rearrange("p (c i t) -> p c t i", c=P, i=4, t=4),
                in_=src.rearrange("p t (c i) -> p c t i", c=P, i=4),
            )

        def x1_quant(gp, ch):
            c = gp * N + ch * 512
            nc.vector.quantize_mx(out=x1c[:, c:c + 512].bitcast(FP8X4), scales=x1s[:, c:c + 512], in_=x1g[(gp, ch)][:])

        def lap_late():
            for a in (2, 3):
                bank = lap_bank(a, 0)
                lap_copy(s_copy, a, 0, bank)
                bank = lap_bank(a, 1)
                lap_copy(v_copy, a, 1, bank)
            lap_quant(2)
            lap_quant(3)

        pairs = [(0, 0), (0, 1), (1, 0), (1, 1)]
        for i, (gp, half) in enumerate(pairs):
            for t in range(4):
                for cc in range(2):
                    s1_tasks(gp, 2 * half + cc, (t,))
                if i == 0:
                    store_rows(0, x1sb[(gp, half)], gp, half, t, 1)
                elif t % 2 == 1:
                    store_rows(0, x1sb[(gp, half)], gp, half, t - 1, 2)
                if i == LAP_AT[0] and t == LAP_AT[1]:
                    lap_late()
            if i < 3:
                for cc in range(2):
                    regroup(gp, 2 * half + cc, v_copy)
                for cc in range(2):
                    x1_quant(gp, 2 * half + cc)

        def s2_evict(i, mt, ch, bank, res):
            a, e = mt // 2, mt % 2
            t = 2 * (a % 2) + e
            x0t = x0g[a // 2][:].rearrange("q (n t) -> q n t", t=4)[:, ch * 512:(ch + 1) * 512, t]
            if i in SG:
                nc.scalar.mul(out=res, in_=bank[:], mul=2.0)
                nc.gpsimd.tensor_tensor(out=res, in0=res, in1=x0t, op=ALU.subtract)
            else:
                nc.vector.scalar_tensor_tensor(out=res, in0=bank[:], scalar=2.0, in1=x0t, op0=ALU.mult, op1=ALU.subtract)

        regroup(1, 2, s_copy)
        regroup(1, 3, s_copy)
        i = 0
        for half in range(2):
            for gp in range(2):
                unit = big.tile([P, 4096], F32, name="unit", tag="big")
                last = half == 1 and gp == 1
                for t in range(4):
                    mt = 4 * gp + t
                    for cc in range(2):
                        ch = 2 * half + cc
                        bank = new_bank()
                        for g in range(2):
                            mx_pass(bank, mt // 2, mt % 2, g, x1c, x1s, ch)
                        c = t * 1024 + cc * 512
                        s2_evict(i, mt, ch, bank, unit[:, c:c + 512])
                        i += 1
                        if last and t == 3:
                            store_rows(1, unit, gp, half, t, 1, cc * 512, (cc + 1) * 512)
                    if last and t == 2:
                        store_rows(1, unit, gp, half, t, 1)
                    elif t % 2 == 1 and not (last and t == 3):
                        store_rows(1, unit, gp, half, t - 1, 2)
                    if half == 0 and mt == 3:
                        x1_quant(1, 2)
                    if half == 0 and mt == 5:
                        x1_quant(1, 3)
